import numpy as np
import ml_dtypes

BF16 = ml_dtypes.bfloat16


def bf(x):
    return np.asarray(x, np.float32).astype(BF16)


def f32(x):
    return np.asarray(x, np.float32)


def f64(x):
    return np.asarray(x).astype(np.float64)


def striped(idx):
    return np.tile(idx.reshape(-1, 16).T, (8, 1))


C, L, D, S, N = 256, 4, 256, 4096, 2048


def setup_inputs():
    return {"x": bf(np.random.standard_normal((C, L, D))), "emb": bf(3.0 * np.random.standard_normal((D, N))), "base": f32(0.05 * np.random.random((C, S))), "offs": striped(np.random.permutation(S)[:N])}


def reference(x, emb, base, offs):
    idx = offs[:16].T.reshape(-1)
    q = np.maximum(f64(x).max(axis=1), 0.0)
    norm = np.sqrt((q * q).sum(axis=1, keepdims=True))
    logit = (q @ f64(emb)) / norm
    e = np.exp(logit - logit.max(axis=1, keepdims=True))
    out = f64(base).copy()
    out[:, idx] = e * (1.0 / e.sum(axis=1, keepdims=True))
    return out

@@ -1,0 +1,137 @@
+import concourse.mybir as mybir
+from concourse.masks import make_identity
+
+FLOPS = 2 * 256 * 256 * 2048
+
+BF16, F32, U16 = mybir.dt.bfloat16, mybir.dt.float32, mybir.dt.uint16
+Alu = mybir.AluOpType
+Act = mybir.ActivationFunctionType
+FREE = mybir.AxisListType.X
+
+P = 128
+BANK = 512
+PSUM_BANKS = 8
+PIECE = 1024
+
+
+def tile_conceptembedmodel_kernel(tc, x, emb, base, offs, out):
+    nc = tc.nc
+    n_samples, n_pos, n_feat = x.shape
+    n_cand = emb.shape[1]
+    n_concepts = base.shape[1]
+    assert n_pos == 4
+    blocks = n_samples // P
+    slabs = n_feat // P
+    banks = n_cand // BANK
+    pieces = n_cand // PIECE
+
+    with (
+        tc.tile_pool(name="held", bufs=1) as held,
+        tc.tile_pool(name="per_block", bufs=blocks) as per_block,
+        tc.psum_pool(name="psum", bufs=PSUM_BANKS) as psum,
+    ):
+        x_blk = [per_block.tile([P, n_pos, n_feat], BF16, name="x_blk") for b in range(blocks)]
+        emb_bank = [held.tile([P, slabs, BANK], BF16, name=f"emb_bank{j}") for j in range(banks)]
+        offsets = held.tile([P, n_cand // 16], U16, name="offsets")
+        window = [per_block.tile([P, n_concepts], F32, name="window") for b in range(blocks)]
+
+        for b in range(blocks):
+            nc.sync.dma_start(x_blk[b][:], x[b * P : (b + 1) * P])
+        emb_by_slab = emb.rearrange("(k p) n -> p k n", p=P)
+        for j in range(banks):
+            nc.sync.dma_start(emb_bank[j][:], emb_by_slab[:, :, j * BANK : (j + 1) * BANK])
+        nc.sync.dma_start(offsets[:], offs)
+        for b in range(blocks):
+            nc.sync.dma_start(window[b][:], base[b * P : (b + 1) * P, :])
+
+        identity = held.tile([P, P], BF16, name="identity")
+        make_identity(nc, identity[:])
+        minus_half = held.tile([P, 1], F32, name="minus_half")
+        nc.gpsimd.memset(minus_half[:], -0.5)
+        ones = held.tile([P, PIECE], F32, name="ones")
+        nc.gpsimd.memset(ones[:], 1.0)
+
+        q = []
+        for b in range(blocks):
+            pair_max = per_block.tile([P, 2, n_feat], BF16, name="pair_max")
+            nc.vector.tensor_tensor(pair_max[:], x_blk[b][:, 0:2, :], x_blk[b][:, 2:4, :], Alu.max)
+            q_b = per_block.tile([P, n_feat], BF16, name="q_b")
+            nc.vector.scalar_tensor_tensor(
+                out=q_b[:], in0=pair_max[:, 0, :], scalar=0.0, in1=pair_max[:, 1, :],
+                op0=Alu.max, op1=Alu.max,
+            )
+            q.append(q_b)
+
+        q_flip_ps = psum.tile([P, blocks, slabs, P], BF16, name="q_flip_ps", tag="bank")
+        q_flip = held.tile([P, blocks, slabs, P], BF16, name="q_flip")
+
+        def flip(b):
+            for k in range(slabs):
+                nc.tensor.transpose(q_flip_ps[:, b, k, :], q[b][:, k * P : (k + 1) * P], identity[:])
+            nc.scalar.copy(q_flip[:, b], q_flip_ps[:, b])
+
+        flip(0)
+
+        inv_norm = []
+        for b in range(blocks):
+            squares = per_block.tile([P, n_feat], F32, name="squares")
+            sum_sq = per_block.tile([P, 1], F32, name="sum_sq")
+            nc.scalar.activation(out=squares[:], in_=q[b][:], func=Act.Square, accum_out=sum_sq[:])
+            inv_norm_b = per_block.tile([P, 1], F32, name="inv_norm_b")
+            nc.gpsimd.tensor_tensor(inv_norm_b[:], sum_sq[:], minus_half[:], Alu.pow)
+            inv_norm.append(inv_norm_b)
+
+        expd = []
+        bank_sum = []
+        for b in range(blocks):
+            raw = []
+            bank_max = per_block.tile([P, banks], F32, name="bank_max")
+            for j in range(banks):
+                raw_j = psum.tile([P, BANK], F32, name="raw_j", tag="bank")
+                for k in range(slabs):
+                    nc.tensor.matmul(
+                        raw_j[:], q_flip[:, b, k, :], emb_bank[j][:, k, :],
+                        start=(k == 0), stop=(k == slabs - 1),
+                    )
+                nc.vector.reduce_max(out=bank_max[:, j : j + 1], in_=raw_j[:], axis=FREE)
+                raw.append(raw_j)
+                if j == 0 and b + 1 < blocks:
+                    flip(b + 1)
+
+            raw_max = per_block.tile([P, 1], F32, name="raw_max")
+            nc.vector.reduce_max(out=raw_max[:], in_=bank_max[:], axis=FREE)
+            shift = per_block.tile([P, 1], F32, name="shift")
+            nc.vector.tensor_scalar(
+                out=shift[:], in0=raw_max[:], scalar1=inv_norm[b][:, 0:1], scalar2=-1.0,
+                op0=Alu.mult, op1=Alu.mult,
+            )
+
+            expd_b = per_block.tile([P, n_cand], F32, name="expd_b")
+            bank_sum_b = per_block.tile([P, banks], F32, name="bank_sum_b")
+            for j in range(banks):
+                nc.scalar.activation(
+                    out=expd_b[:, j * BANK : (j + 1) * BANK], in_=raw[j][:], func=Act.Exp,
+                    bias=shift[:, 0:1], scale=inv_norm[b][:, 0:1],
+                    accum_out=bank_sum_b[:, j : j + 1],
+                )
+            expd.append(expd_b)
+            bank_sum.append(bank_sum_b)
+
+        for b in range(blocks):
+            total = per_block.tile([P, 1], F32, name="total")
+            nc.vector.reduce_sum(out=total[:], in_=bank_sum[b][:], axis=FREE)
+            inv_total = per_block.tile([P, 1], F32, name="inv_total")
+            nc.vector.reciprocal(inv_total[:], total[:])
+            inv_spread = per_block.tile([P, PIECE], F32, name="inv_spread")
+            if b == 0:
+                nc.vector.tensor_scalar_mul(out=inv_spread[:], in0=ones[:], scalar1=inv_total[:, 0:1])
+            else:
+                nc.scalar.activation(out=inv_spread[:], in_=ones[:], func=Act.Copy, scale=inv_total[:, 0:1])
+            for h in range(pieces):
+                nc.vector.tensor_tensor(
+                    window[b][:].indirect(offsets[:, h * (PIECE // 16) : (h + 1) * (PIECE // 16)]),
+                    expd[b][:, h * PIECE : (h + 1) * PIECE],
+                    inv_spread[:],
+                    Alu.mult,
+                )
+            nc.sync.dma_start(out[b * P : (b + 1) * P, :], window[b][:])

@@ -12,6 +12,7 @@ P = 128
 BANK = 512
 PSUM_BANKS = 8
 PIECE = 1024
+WARM_UP = 8
 
 
 def tile_conceptembedmodel_kernel(tc, x, emb, base, offs, out):
@@ -48,8 +49,16 @@ def tile_conceptembedmodel_kernel(tc, x, emb, base, offs, out):
         make_identity(nc, identity[:])
         minus_half = held.tile([P, 1], F32, name="minus_half")
         nc.gpsimd.memset(minus_half[:], -0.5)
+        minus_one = held.tile([P, 1], F32, name="minus_one")
+        nc.gpsimd.memset(minus_one[:], -1.0)
         ones = held.tile([P, PIECE], F32, name="ones")
         nc.gpsimd.memset(ones[:], 1.0)
+
+        zeros = held.tile([P, BANK], BF16, name="zeros")
+        nc.vector.memset(zeros[:], 0.0)
+        warm_ps = psum.tile([P, BANK], F32, name="warm_ps", tag="bank")
+        for i in range(WARM_UP):
+            nc.tensor.matmul(warm_ps[:], zeros[:, 0:P], zeros[:], start=True, stop=True)
 
         q = []
         for b in range(blocks):
@@ -119,13 +128,18 @@ def tile_conceptembedmodel_kernel(tc, x, emb, base, offs, out):
 
         for b in range(blocks):
             total = per_block.tile([P, 1], F32, name="total")
-            nc.vector.reduce_sum(out=total[:], in_=bank_sum[b][:], axis=FREE)
             inv_total = per_block.tile([P, 1], F32, name="inv_total")
-            nc.vector.reciprocal(inv_total[:], total[:])
             inv_spread = per_block.tile([P, PIECE], F32, name="inv_spread")
             if b == 0:
+                nc.vector.reduce_sum(out=total[:], in_=bank_sum[b][:], axis=FREE)
+                nc.vector.reciprocal(inv_total[:], total[:])
                 nc.vector.tensor_scalar_mul(out=inv_spread[:], in0=ones[:], scalar1=inv_total[:, 0:1])
             else:
+                bank_sum_copy = per_block.tile([P, banks], F32, name="bank_sum_copy")
+                nc.scalar.activation(
+                    out=bank_sum_copy[:], in_=bank_sum[b][:], func=Act.Copy, accum_out=total[:]
+                )
+                nc.gpsimd.tensor_tensor(inv_total[:], total[:], minus_one[:], Alu.pow)
                 nc.scalar.activation(out=inv_spread[:], in_=ones[:], func=Act.Copy, scale=inv_total[:, 0:1])
             for h in range(pieces):
                 nc.vector.tensor_tensor(

@@ -25,6 +25,7 @@ def tile_conceptembedmodel_kernel(tc, x, emb, base, offs, out):
     slabs = n_feat // P
     banks = n_cand // BANK
     pieces = n_cand // PIECE
+    banks_a_piece = PIECE // BANK
 
     with (
         tc.tile_pool(name="held", bufs=1) as held,
@@ -51,7 +52,7 @@ def tile_conceptembedmodel_kernel(tc, x, emb, base, offs, out):
         nc.gpsimd.memset(minus_half[:], -0.5)
         minus_one = held.tile([P, 1], F32, name="minus_one")
         nc.gpsimd.memset(minus_one[:], -1.0)
-        ones = held.tile([P, PIECE], F32, name="ones")
+        ones = held.tile([P, BANK], F32, name="ones")
         nc.gpsimd.memset(ones[:], 1.0)
 
         zeros = held.tile([P, BANK], BF16, name="zeros")
@@ -91,10 +92,12 @@ def tile_conceptembedmodel_kernel(tc, x, emb, base, offs, out):
             inv_norm.append(inv_norm_b)
 
         expd = []
-        bank_sum = []
+        factor_spread = []
         for b in range(blocks):
-            raw = []
-            bank_max = per_block.tile([P, banks], F32, name="bank_max")
+            expd_b = per_block.tile([P, n_cand], F32, name="expd_b")
+            raw_top = per_block.tile([P, banks], F32, name="raw_top")
+            neg_top = per_block.tile([P, banks], F32, name="neg_top")
+            bank_sum = per_block.tile([P, banks], F32, name="bank_sum")
             for j in range(banks):
                 raw_j = psum.tile([P, BANK], F32, name="raw_j", tag="bank")
                 for k in range(slabs):
@@ -102,50 +105,66 @@ def tile_conceptembedmodel_kernel(tc, x, emb, base, offs, out):
                         raw_j[:], q_flip[:, b, k, :], emb_bank[j][:, k, :],
                         start=(k == 0), stop=(k == slabs - 1),
                     )
-                nc.vector.reduce_max(out=bank_max[:, j : j + 1], in_=raw_j[:], axis=FREE)
-                raw.append(raw_j)
+                nc.vector.reduce_max(out=raw_top[:, j : j + 1], in_=raw_j[:], axis=FREE)
+                nc.vector.tensor_scalar(
+                    out=neg_top[:, j : j + 1], in0=raw_top[:, j : j + 1],
+                    scalar1=inv_norm[b][:, 0:1], scalar2=-1.0, op0=Alu.mult, op1=Alu.mult,
+                )
+                nc.scalar.activation(
+                    out=expd_b[:, j * BANK : (j + 1) * BANK], in_=raw_j[:], func=Act.Exp,
+                    bias=neg_top[:, j : j + 1], scale=inv_norm[b][:, 0:1],
+                    accum_out=bank_sum[:, j : j + 1],
+                )
                 if j == 0 and b + 1 < blocks:
                     flip(b + 1)
 
-            raw_max = per_block.tile([P, 1], F32, name="raw_max")
-            nc.vector.reduce_max(out=raw_max[:], in_=bank_max[:], axis=FREE)
-            shift = per_block.tile([P, 1], F32, name="shift")
-            nc.vector.tensor_scalar(
-                out=shift[:], in0=raw_max[:], scalar1=inv_norm[b][:, 0:1], scalar2=-1.0,
-                op0=Alu.mult, op1=Alu.mult,
+            neg_row_top = per_block.tile([P, 1], F32, name="neg_row_top")
+            nc.vector.tensor_reduce(out=neg_row_top[:], in_=neg_top[:], axis=FREE, op=Alu.min)
+            rescale = per_block.tile([P, banks], F32, name="rescale")
+            nc.scalar.activation(
+                out=rescale[:], in_=neg_top[:], func=Act.Exp, bias=neg_row_top[:, 0:1], scale=-1.0
             )
 
-            expd_b = per_block.tile([P, n_cand], F32, name="expd_b")
-            bank_sum_b = per_block.tile([P, banks], F32, name="bank_sum_b")
-            for j in range(banks):
-                nc.scalar.activation(
-                    out=expd_b[:, j * BANK : (j + 1) * BANK], in_=raw[j][:], func=Act.Exp,
-                    bias=shift[:, 0:1], scale=inv_norm[b][:, 0:1],
-                    accum_out=bank_sum_b[:, j : j + 1],
-                )
-            expd.append(expd_b)
-            bank_sum.append(bank_sum_b)
-
-        for b in range(blocks):
+            first = b == 0
+            weighted = per_block.tile([P, banks], F32, name="weighted")
             total = per_block.tile([P, 1], F32, name="total")
             inv_total = per_block.tile([P, 1], F32, name="inv_total")
-            inv_spread = per_block.tile([P, PIECE], F32, name="inv_spread")
-            if b == 0:
-                nc.vector.reduce_sum(out=total[:], in_=bank_sum[b][:], axis=FREE)
+            if first:
+                nc.vector.tensor_tensor(weighted[:], rescale[:], bank_sum[:], Alu.mult)
+                nc.vector.reduce_sum(out=total[:], in_=weighted[:], axis=FREE)
                 nc.vector.reciprocal(inv_total[:], total[:])
-                nc.vector.tensor_scalar_mul(out=inv_spread[:], in0=ones[:], scalar1=inv_total[:, 0:1])
             else:
-                bank_sum_copy = per_block.tile([P, banks], F32, name="bank_sum_copy")
+                nc.gpsimd.tensor_tensor(weighted[:], rescale[:], bank_sum[:], Alu.mult)
+                weighted_copy = per_block.tile([P, banks], F32, name="weighted_copy")
                 nc.scalar.activation(
-                    out=bank_sum_copy[:], in_=bank_sum[b][:], func=Act.Copy, accum_out=total[:]
+                    out=weighted_copy[:], in_=weighted[:], func=Act.Copy, accum_out=total[:]
                 )
                 nc.gpsimd.tensor_tensor(inv_total[:], total[:], minus_one[:], Alu.pow)
-                nc.scalar.activation(out=inv_spread[:], in_=ones[:], func=Act.Copy, scale=inv_total[:, 0:1])
+
+            factor = per_block.tile([P, banks], F32, name="factor")
+            nc.scalar.activation(out=factor[:], in_=rescale[:], func=Act.Copy, scale=inv_total[:, 0:1])
+            factor_spread_b = per_block.tile([P, n_cand], F32, name="factor_spread_b")
+            for j in range(banks):
+                if first and j < banks_a_piece:
+                    nc.vector.tensor_scalar(
+                        out=factor_spread_b[:, j * BANK : (j + 1) * BANK], in0=ones[:],
+                        scalar1=rescale[:, j : j + 1], scalar2=inv_total[:, 0:1],
+                        op0=Alu.mult, op1=Alu.mult,
+                    )
+                else:
+                    nc.scalar.activation(
+                        out=factor_spread_b[:, j * BANK : (j + 1) * BANK], in_=ones[:],
+                        func=Act.Copy, scale=factor[:, j : j + 1],
+                    )
+            expd.append(expd_b)
+            factor_spread.append(factor_spread_b)
+
+        for b in range(blocks):
             for h in range(pieces):
                 nc.vector.tensor_tensor(
                     window[b][:].indirect(offsets[:, h * (PIECE // 16) : (h + 1) * (PIECE // 16)]),
                     expd[b][:, h * PIECE : (h + 1) * PIECE],
-                    inv_spread[:],
+                    factor_spread[b][:, h * PIECE : (h + 1) * PIECE],
                     Alu.mult,
                 )
             nc.sync.dma_start(out[b * P : (b + 1) * P, :], window[b][:])

@@ -12,7 +12,7 @@ P = 128
 BANK = 512
 PSUM_BANKS = 8
 PIECE = 1024
-WARM_UP = 8
+WARM_UP = 5
 
 
 def tile_conceptembedmodel_kernel(tc, x, emb, base, offs, out):
@@ -86,7 +86,10 @@ def tile_conceptembedmodel_kernel(tc, x, emb, base, offs, out):
         for b in range(blocks):
             squares = per_block.tile([P, n_feat], F32, name="squares")
             sum_sq = per_block.tile([P, 1], F32, name="sum_sq")
-            nc.scalar.activation(out=squares[:], in_=q[b][:], func=Act.Square, accum_out=sum_sq[:])
+            nc.vector.scalar_tensor_tensor(
+                out=squares[:], in0=q[b][:], scalar=1.0, in1=q[b][:],
+                op0=Alu.mult, op1=Alu.mult, accum_out=sum_sq[:],
+            )
             inv_norm_b = per_block.tile([P, 1], F32, name="inv_norm_b")
             nc.gpsimd.tensor_tensor(inv_norm_b[:], sum_sq[:], minus_half[:], Alu.pow)
             inv_norm.append(inv_norm_b)

@@ -11,7 +11,7 @@ FREE = mybir.AxisListType.X
 P = 128
 BANK = 512
 PSUM_BANKS = 8
-PIECE = 1024
+FIRST_PIECE = 512
 WARM_UP = 5
 
 
@@ -24,8 +24,7 @@ def tile_conceptembedmodel_kernel(tc, x, emb, base, offs, out):
     blocks = n_samples // P
     slabs = n_feat // P
     banks = n_cand // BANK
-    pieces = n_cand // PIECE
-    banks_a_piece = PIECE // BANK
+    banks_a_piece = FIRST_PIECE // BANK
 
     with (
         tc.tile_pool(name="held", bufs=1) as held,
@@ -163,11 +162,12 @@ def tile_conceptembedmodel_kernel(tc, x, emb, base, offs, out):
             factor_spread.append(factor_spread_b)
 
         for b in range(blocks):
-            for h in range(pieces):
+            cuts = [0, FIRST_PIECE, n_cand] if b == 0 else [0, n_cand]
+            for at, end in zip(cuts[:-1], cuts[1:]):
                 nc.vector.tensor_tensor(
-                    window[b][:].indirect(offsets[:, h * (PIECE // 16) : (h + 1) * (PIECE // 16)]),
-                    expd[b][:, h * PIECE : (h + 1) * PIECE],
-                    factor_spread[b][:, h * PIECE : (h + 1) * PIECE],
+                    window[b][:].indirect(offsets[:, at // 16 : end // 16]),
+                    expd[b][:, at:end],
+                    factor_spread[b][:, at:end],
                     Alu.mult,
                 )
             nc.sync.dma_start(out[b * P : (b + 1) * P, :], window[b][:])

@@ -60,24 +60,23 @@ def tile_conceptembedmodel_kernel(tc, x, emb, base, offs, out):
         for i in range(WARM_UP):
             nc.tensor.matmul(warm_ps[:], zeros[:, 0:P], zeros[:], start=True, stop=True)
 
-        q = []
+        pooled = []
         for b in range(blocks):
             pair_max = per_block.tile([P, 2, n_feat], BF16, name="pair_max")
             nc.vector.tensor_tensor(pair_max[:], x_blk[b][:, 0:2, :], x_blk[b][:, 2:4, :], Alu.max)
-            q_b = per_block.tile([P, n_feat], BF16, name="q_b")
-            nc.vector.scalar_tensor_tensor(
-                out=q_b[:], in0=pair_max[:, 0, :], scalar=0.0, in1=pair_max[:, 1, :],
-                op0=Alu.max, op1=Alu.max,
-            )
-            q.append(q_b)
+            pooled_b = per_block.tile([P, n_feat], BF16, name="pooled_b")
+            nc.vector.tensor_tensor(pooled_b[:], pair_max[:, 0, :], pair_max[:, 1, :], Alu.max)
+            pooled.append(pooled_b)
 
         q_flip_ps = psum.tile([P, blocks, slabs, P], BF16, name="q_flip_ps", tag="bank")
         q_flip = held.tile([P, blocks, slabs, P], BF16, name="q_flip")
 
         def flip(b):
             for k in range(slabs):
-                nc.tensor.transpose(q_flip_ps[:, b, k, :], q[b][:, k * P : (k + 1) * P], identity[:])
-            nc.scalar.copy(q_flip[:, b], q_flip_ps[:, b])
+                nc.tensor.transpose(
+                    q_flip_ps[:, b, k, :], pooled[b][:, k * P : (k + 1) * P], identity[:]
+                )
+            nc.scalar.activation(out=q_flip[:, b], in_=q_flip_ps[:, b], func=Act.Relu)
 
         flip(0)
 
@@ -86,8 +85,8 @@ def tile_conceptembedmodel_kernel(tc, x, emb, base, offs, out):
             squares = per_block.tile([P, n_feat], F32, name="squares")
             sum_sq = per_block.tile([P, 1], F32, name="sum_sq")
             nc.vector.scalar_tensor_tensor(
-                out=squares[:], in0=q[b][:], scalar=1.0, in1=q[b][:],
-                op0=Alu.mult, op1=Alu.mult, accum_out=sum_sq[:],
+                out=squares[:], in0=pooled[b][:], scalar=0.0, in1=pooled[b][:],
+                op0=Alu.max, op1=Alu.mult, accum_out=sum_sq[:],
             )
             inv_norm_b = per_block.tile([P, 1], F32, name="inv_norm_b")
             nc.gpsimd.tensor_tensor(inv_norm_b[:], sum_sq[:], minus_half[:], Alu.pow)
@@ -132,8 +131,10 @@ def tile_conceptembedmodel_kernel(tc, x, emb, base, offs, out):
             total = per_block.tile([P, 1], F32, name="total")
             inv_total = per_block.tile([P, 1], F32, name="inv_total")
             if first:
-                nc.vector.tensor_tensor(weighted[:], rescale[:], bank_sum[:], Alu.mult)
-                nc.vector.reduce_sum(out=total[:], in_=weighted[:], axis=FREE)
+                nc.vector.scalar_tensor_tensor(
+                    out=weighted[:], in0=rescale[:], scalar=1.0, in1=bank_sum[:],
+                    op0=Alu.mult, op1=Alu.mult, accum_out=total[:],
+                )
                 nc.vector.reciprocal(inv_total[:], total[:])
             else:
                 nc.gpsimd.tensor_tensor(weighted[:], rescale[:], bank_sum[:], Alu.mult)

@@ -12,7 +12,7 @@ P = 128
 BANK = 512
 PSUM_BANKS = 8
 FIRST_PIECE = 512
-WARM_UP = 5
+WARM_UP = 4
 
 
 def tile_conceptembedmodel_kernel(tc, x, emb, base, offs, out):
@@ -49,8 +49,6 @@ def tile_conceptembedmodel_kernel(tc, x, emb, base, offs, out):
         make_identity(nc, identity[:])
         minus_half = held.tile([P, 1], F32, name="minus_half")
         nc.gpsimd.memset(minus_half[:], -0.5)
-        minus_one = held.tile([P, 1], F32, name="minus_one")
-        nc.gpsimd.memset(minus_one[:], -1.0)
         ones = held.tile([P, BANK], F32, name="ones")
         nc.gpsimd.memset(ones[:], 1.0)
 
@@ -63,22 +61,30 @@ def tile_conceptembedmodel_kernel(tc, x, emb, base, offs, out):
         pooled = []
         for b in range(blocks):
             pair_max = per_block.tile([P, 2, n_feat], BF16, name="pair_max")
-            nc.vector.tensor_tensor(pair_max[:], x_blk[b][:, 0:2, :], x_blk[b][:, 2:4, :], Alu.max)
             pooled_b = per_block.tile([P, n_feat], BF16, name="pooled_b")
-            nc.vector.tensor_tensor(pooled_b[:], pair_max[:, 0, :], pair_max[:, 1, :], Alu.max)
+            width = P if b == 0 else n_feat
+            pieces = [slice(at, at + width) for at in range(0, n_feat, width)]
+            for d in pieces:
+                nc.vector.tensor_tensor(
+                    pair_max[:, :, d], x_blk[b][:, 0:2, d], x_blk[b][:, 2:4, d], Alu.max
+                )
+            for d in pieces:
+                nc.vector.tensor_tensor(pooled_b[:, d], pair_max[:, 0, d], pair_max[:, 1, d], Alu.max)
             pooled.append(pooled_b)
 
-        q_flip_ps = psum.tile([P, blocks, slabs, P], BF16, name="q_flip_ps", tag="bank")
         q_flip = held.tile([P, blocks, slabs, P], BF16, name="q_flip")
 
-        def flip(b):
-            for k in range(slabs):
-                nc.tensor.transpose(
-                    q_flip_ps[:, b, k, :], pooled[b][:, k * P : (k + 1) * P], identity[:]
-                )
-            nc.scalar.activation(out=q_flip[:, b], in_=q_flip_ps[:, b], func=Act.Relu)
+        def flip(b, slabs_at_once):
+            for k0 in range(0, slabs, slabs_at_once):
+                ks = slice(k0, k0 + slabs_at_once)
+                q_flip_ps = psum.tile([P, slabs, P], BF16, name="q_flip_ps", tag="bank")
+                for k in range(k0, k0 + slabs_at_once):
+                    nc.tensor.transpose(
+                        q_flip_ps[:, k, :], pooled[b][:, k * P : (k + 1) * P], identity[:]
+                    )
+                nc.scalar.activation(out=q_flip[:, b, ks], in_=q_flip_ps[:, ks], func=Act.Relu)
 
-        flip(0)
+        flip(0, 1)
 
         inv_norm = []
         for b in range(blocks):
@@ -95,69 +101,91 @@ def tile_conceptembedmodel_kernel(tc, x, emb, base, offs, out):
         expd = []
         factor_spread = []
         for b in range(blocks):
+            first = b == 0
             expd_b = per_block.tile([P, n_cand], F32, name="expd_b")
             raw_top = per_block.tile([P, banks], F32, name="raw_top")
             neg_top = per_block.tile([P, banks], F32, name="neg_top")
             bank_sum = per_block.tile([P, banks], F32, name="bank_sum")
+            inv_total = per_block.tile([P, 1], F32, name="inv_total")
+            factor_spread_b = per_block.tile([P, n_cand], F32, name="factor_spread_b")
+            raw = []
+
+            def exponentials(j, neg_shift):
+                nc.scalar.activation(
+                    out=expd_b[:, j * BANK : (j + 1) * BANK], in_=raw[j][:], func=Act.Exp,
+                    bias=neg_shift, scale=inv_norm[b][:, 0:1], accum_out=bank_sum[:, j : j + 1],
+                )
+
             for j in range(banks):
                 raw_j = psum.tile([P, BANK], F32, name="raw_j", tag="bank")
+                raw.append(raw_j)
                 for k in range(slabs):
                     nc.tensor.matmul(
                         raw_j[:], q_flip[:, b, k, :], emb_bank[j][:, k, :],
                         start=(k == 0), stop=(k == slabs - 1),
                     )
                 nc.vector.reduce_max(out=raw_top[:, j : j + 1], in_=raw_j[:], axis=FREE)
-                nc.vector.tensor_scalar(
-                    out=neg_top[:, j : j + 1], in0=raw_top[:, j : j + 1],
-                    scalar1=inv_norm[b][:, 0:1], scalar2=-1.0, op0=Alu.mult, op1=Alu.mult,
-                )
-                nc.scalar.activation(
-                    out=expd_b[:, j * BANK : (j + 1) * BANK], in_=raw_j[:], func=Act.Exp,
-                    bias=neg_top[:, j : j + 1], scale=inv_norm[b][:, 0:1],
-                    accum_out=bank_sum[:, j : j + 1],
-                )
+                if first:
+                    nc.vector.tensor_scalar(
+                        out=neg_top[:, j : j + 1], in0=raw_top[:, j : j + 1],
+                        scalar1=inv_norm[b][:, 0:1], scalar2=-1.0, op0=Alu.mult, op1=Alu.mult,
+                    )
+                    exponentials(j, neg_top[:, j : j + 1])
                 if j == 0 and b + 1 < blocks:
-                    flip(b + 1)
+                    flip(b + 1, slabs)
 
-            neg_row_top = per_block.tile([P, 1], F32, name="neg_row_top")
-            nc.vector.tensor_reduce(out=neg_row_top[:], in_=neg_top[:], axis=FREE, op=Alu.min)
-            rescale = per_block.tile([P, banks], F32, name="rescale")
-            nc.scalar.activation(
-                out=rescale[:], in_=neg_top[:], func=Act.Exp, bias=neg_row_top[:, 0:1], scale=-1.0
-            )
-
-            first = b == 0
-            weighted = per_block.tile([P, banks], F32, name="weighted")
-            total = per_block.tile([P, 1], F32, name="total")
-            inv_total = per_block.tile([P, 1], F32, name="inv_total")
             if first:
+                neg_row_top = per_block.tile([P, 1], F32, name="neg_row_top")
+                nc.vector.tensor_reduce(out=neg_row_top[:], in_=neg_top[:], axis=FREE, op=Alu.min)
+                rescale = per_block.tile([P, banks], F32, name="rescale")
+                nc.scalar.activation(
+                    out=rescale[:], in_=neg_top[:], func=Act.Exp, bias=neg_row_top[:, 0:1], scale=-1.0
+                )
+                weighted = per_block.tile([P, banks], F32, name="weighted")
+                total = per_block.tile([P, 1], F32, name="total")
                 nc.vector.scalar_tensor_tensor(
                     out=weighted[:], in0=rescale[:], scalar=1.0, in1=bank_sum[:],
                     op0=Alu.mult, op1=Alu.mult, accum_out=total[:],
                 )
                 nc.vector.reciprocal(inv_total[:], total[:])
-            else:
-                nc.gpsimd.tensor_tensor(weighted[:], rescale[:], bank_sum[:], Alu.mult)
-                weighted_copy = per_block.tile([P, banks], F32, name="weighted_copy")
-                nc.scalar.activation(
-                    out=weighted_copy[:], in_=weighted[:], func=Act.Copy, accum_out=total[:]
-                )
-                nc.gpsimd.tensor_tensor(inv_total[:], total[:], minus_one[:], Alu.pow)
 
-            factor = per_block.tile([P, banks], F32, name="factor")
-            nc.scalar.activation(out=factor[:], in_=rescale[:], func=Act.Copy, scale=inv_total[:, 0:1])
-            factor_spread_b = per_block.tile([P, n_cand], F32, name="factor_spread_b")
-            for j in range(banks):
-                if first and j < banks_a_piece:
-                    nc.vector.tensor_scalar(
-                        out=factor_spread_b[:, j * BANK : (j + 1) * BANK], in0=ones[:],
-                        scalar1=rescale[:, j : j + 1], scalar2=inv_total[:, 0:1],
-                        op0=Alu.mult, op1=Alu.mult,
-                    )
-                else:
+                factor = per_block.tile([P, banks], F32, name="factor")
+                nc.scalar.activation(
+                    out=factor[:], in_=rescale[:], func=Act.Copy, scale=inv_total[:, 0:1]
+                )
+                for j in range(banks):
+                    if j < banks_a_piece:
+                        nc.vector.tensor_scalar(
+                            out=factor_spread_b[:, j * BANK : (j + 1) * BANK], in0=ones[:],
+                            scalar1=rescale[:, j : j + 1], scalar2=inv_total[:, 0:1],
+                            op0=Alu.mult, op1=Alu.mult,
+                        )
+                    else:
+                        nc.scalar.activation(
+                            out=factor_spread_b[:, j * BANK : (j + 1) * BANK], in_=ones[:],
+                            func=Act.Copy, scale=factor[:, j : j + 1],
+                        )
+            else:
+                neg_raw_row_top = per_block.tile([P, 1], F32, name="neg_raw_row_top")
+                nc.vector.reduce_max(out=neg_raw_row_top[:], in_=raw_top[:], axis=FREE, negate=True)
+                neg_row_top = per_block.tile([P, 1], F32, name="neg_row_top")
+                nc.scalar.activation(
+                    out=neg_row_top[:], in_=neg_raw_row_top[:], func=Act.Copy, scale=inv_norm[b][:, 0:1]
+                )
+                for j in range(banks):
+                    exponentials(j, neg_row_top[:, 0:1])
+                sum_copy = per_block.tile([P, banks], F32, name="sum_copy")
+                total = per_block.tile([P, 1], F32, name="total")
+                nc.scalar.activation(
+                    out=sum_copy[:], in_=bank_sum[:], func=Act.Copy, accum_out=total[:]
+                )
+                log_total = per_block.tile([P, 1], F32, name="log_total")
+                nc.scalar.activation(out=log_total[:], in_=total[:], func=Act.Ln)
+                nc.scalar.activation(out=inv_total[:], in_=log_total[:], func=Act.Exp, scale=-1.0)
+                for j in range(banks):
                     nc.scalar.activation(
                         out=factor_spread_b[:, j * BANK : (j + 1) * BANK], in_=ones[:],
-                        func=Act.Copy, scale=factor[:, j : j + 1],
+                        func=Act.Copy, scale=inv_total[:, 0:1],
                     )
             expd.append(expd_b)
             factor_spread.append(factor_spread_b)

@@ -103,8 +103,7 @@ def tile_conceptembedmodel_kernel(tc, x, emb, base, offs, out):
         for b in range(blocks):
             first = b == 0
             expd_b = per_block.tile([P, n_cand], F32, name="expd_b")
-            raw_top = per_block.tile([P, banks], F32, name="raw_top")
-            neg_top = per_block.tile([P, banks], F32, name="neg_top")
+            neg_raw_top = per_block.tile([P, banks], F32, name="neg_raw_top")
             bank_sum = per_block.tile([P, banks], F32, name="bank_sum")
             inv_total = per_block.tile([P, 1], F32, name="inv_total")
             factor_spread_b = per_block.tile([P, n_cand], F32, name="factor_spread_b")
@@ -124,17 +123,23 @@ def tile_conceptembedmodel_kernel(tc, x, emb, base, offs, out):
                         raw_j[:], q_flip[:, b, k, :], emb_bank[j][:, k, :],
                         start=(k == 0), stop=(k == slabs - 1),
                     )
-                nc.vector.reduce_max(out=raw_top[:, j : j + 1], in_=raw_j[:], axis=FREE)
-                if first:
-                    nc.vector.tensor_scalar(
-                        out=neg_top[:, j : j + 1], in0=raw_top[:, j : j + 1],
-                        scalar1=inv_norm[b][:, 0:1], scalar2=-1.0, op0=Alu.mult, op1=Alu.mult,
-                    )
-                    exponentials(j, neg_top[:, j : j + 1])
+                nc.vector.reduce_max(
+                    out=neg_raw_top[:, j : j + 1], in_=raw_j[:], axis=FREE, negate=True
+                )
                 if j == 0 and b + 1 < blocks:
                     flip(b + 1, slabs)
 
             if first:
+                neg_top = per_block.tile([P, banks], F32, name="neg_top")
+                for lo, hi in ((0, 1), (1, banks - 1), (banks - 1, banks)):
+                    nc.scalar.activation(
+                        out=neg_top[:, lo:hi], in_=neg_raw_top[:, lo:hi], func=Act.Copy,
+                        scale=inv_norm[b][:, 0:1],
+                    )
+                    if hi < banks:
+                        exponentials(lo, neg_top[:, lo : lo + 1])
+                for j in range(2, banks):
+                    exponentials(j, neg_top[:, j : j + 1])
                 neg_row_top = per_block.tile([P, 1], F32, name="neg_row_top")
                 nc.vector.tensor_reduce(out=neg_row_top[:], in_=neg_top[:], axis=FREE, op=Alu.min)
                 rescale = per_block.tile([P, banks], F32, name="rescale")
@@ -167,7 +172,7 @@ def tile_conceptembedmodel_kernel(tc, x, emb, base, offs, out):
                         )
             else:
                 neg_raw_row_top = per_block.tile([P, 1], F32, name="neg_raw_row_top")
-                nc.vector.reduce_max(out=neg_raw_row_top[:], in_=raw_top[:], axis=FREE, negate=True)
+                nc.vector.tensor_reduce(out=neg_raw_row_top[:], in_=neg_raw_top[:], axis=FREE, op=Alu.min)
                 neg_row_top = per_block.tile([P, 1], F32, name="neg_row_top")
                 nc.scalar.activation(
                     out=neg_row_top[:], in_=neg_raw_row_top[:], func=Act.Copy, scale=inv_norm[b][:, 0:1]

import concourse.mybir as mybir
from concourse.masks import make_identity

FLOPS = 2 * 256 * 256 * 2048

BF16, F32, U16 = mybir.dt.bfloat16, mybir.dt.float32, mybir.dt.uint16
Alu = mybir.AluOpType
Act = mybir.ActivationFunctionType
FREE = mybir.AxisListType.X

P = 128
BANK = 512
PSUM_BANKS = 8
FIRST_PIECE = 512
WARM_UP = 4


def tile_conceptembedmodel_kernel(tc, x, emb, base, offs, out):
    nc = tc.nc
    n_samples, n_pos, n_feat = x.shape
    n_cand = emb.shape[1]
    n_concepts = base.shape[1]
    assert n_pos == 4
    blocks = n_samples // P
    slabs = n_feat // P
    banks = n_cand // BANK
    banks_a_piece = FIRST_PIECE // BANK

    with (
        tc.tile_pool(name="held", bufs=1) as held,
        tc.tile_pool(name="per_block", bufs=blocks) as per_block,
        tc.psum_pool(name="psum", bufs=PSUM_BANKS) as psum,
    ):
        x_blk = [per_block.tile([P, n_pos, n_feat], BF16, name="x_blk") for b in range(blocks)]
        emb_bank = [held.tile([P, slabs, BANK], BF16, name=f"emb_bank{j}") for j in range(banks)]
        offsets = held.tile([P, n_cand // 16], U16, name="offsets")
        window = [per_block.tile([P, n_concepts], F32, name="window") for b in range(blocks)]

        for b in range(blocks):
            nc.sync.dma_start(x_blk[b][:], x[b * P : (b + 1) * P])
        emb_by_slab = emb.rearrange("(k p) n -> p k n", p=P)
        for j in range(banks):
            nc.sync.dma_start(emb_bank[j][:], emb_by_slab[:, :, j * BANK : (j + 1) * BANK])
        nc.sync.dma_start(offsets[:], offs)
        for b in range(blocks):
            nc.sync.dma_start(window[b][:], base[b * P : (b + 1) * P, :])

        identity = held.tile([P, P], BF16, name="identity")
        make_identity(nc, identity[:])
        minus_half = held.tile([P, 1], F32, name="minus_half")
        nc.gpsimd.memset(minus_half[:], -0.5)
        ones = held.tile([P, BANK], F32, name="ones")
        nc.gpsimd.memset(ones[:], 1.0)

        zeros = held.tile([P, BANK], BF16, name="zeros")
        nc.vector.memset(zeros[:], 0.0)
        warm_ps = psum.tile([P, BANK], F32, name="warm_ps", tag="bank")
        for i in range(WARM_UP):
            nc.tensor.matmul(warm_ps[:], zeros[:, 0:P], zeros[:], start=True, stop=True)

        pooled = []
        for b in range(blocks):
            pair_max = per_block.tile([P, 2, n_feat], BF16, name="pair_max")
            pooled_b = per_block.tile([P, n_feat], BF16, name="pooled_b")
            width = P if b == 0 else n_feat
            pieces = [slice(at, at + width) for at in range(0, n_feat, width)]
            for d in pieces:
                nc.vector.tensor_tensor(
                    pair_max[:, :, d], x_blk[b][:, 0:2, d], x_blk[b][:, 2:4, d], Alu.max
                )
            for d in pieces:
                nc.vector.tensor_tensor(pooled_b[:, d], pair_max[:, 0, d], pair_max[:, 1, d], Alu.max)
            pooled.append(pooled_b)

        q_flip = held.tile([P, blocks, slabs, P], BF16, name="q_flip")

        def flip(b, slabs_at_once):
            for k0 in range(0, slabs, slabs_at_once):
                ks = slice(k0, k0 + slabs_at_once)
                q_flip_ps = psum.tile([P, slabs, P], BF16, name="q_flip_ps", tag="bank")
                for k in range(k0, k0 + slabs_at_once):
                    nc.tensor.transpose(
                        q_flip_ps[:, k, :], pooled[b][:, k * P : (k + 1) * P], identity[:]
                    )
                nc.scalar.activation(out=q_flip[:, b, ks], in_=q_flip_ps[:, ks], func=Act.Relu)

        flip(0, 1)

        inv_norm = []
        for b in range(blocks):
            squares = per_block.tile([P, n_feat], F32, name="squares")
            sum_sq = per_block.tile([P, 1], F32, name="sum_sq")
            nc.vector.scalar_tensor_tensor(
                out=squares[:], in0=pooled[b][:], scalar=0.0, in1=pooled[b][:],
                op0=Alu.max, op1=Alu.mult, accum_out=sum_sq[:],
            )
            inv_norm_b = per_block.tile([P, 1], F32, name="inv_norm_b")
            nc.gpsimd.tensor_tensor(inv_norm_b[:], sum_sq[:], minus_half[:], Alu.pow)
            inv_norm.append(inv_norm_b)

        expd = []
        factor_spread = []
        for b in range(blocks):
            first = b == 0
            expd_b = per_block.tile([P, n_cand], F32, name="expd_b")
            neg_raw_top = per_block.tile([P, banks], F32, name="neg_raw_top")
            bank_sum = per_block.tile([P, banks], F32, name="bank_sum")
            inv_total = per_block.tile([P, 1], F32, name="inv_total")
            factor_spread_b = per_block.tile([P, n_cand], F32, name="factor_spread_b")
            raw = []

            def exponentials(j, neg_shift):
                nc.scalar.activation(
                    out=expd_b[:, j * BANK : (j + 1) * BANK], in_=raw[j][:], func=Act.Exp,
                    bias=neg_shift, scale=inv_norm[b][:, 0:1], accum_out=bank_sum[:, j : j + 1],
                )

            for j in range(banks):
                raw_j = psum.tile([P, BANK], F32, name="raw_j", tag="bank")
                raw.append(raw_j)
                for k in range(slabs):
                    nc.tensor.matmul(
                        raw_j[:], q_flip[:, b, k, :], emb_bank[j][:, k, :],
                        start=(k == 0), stop=(k == slabs - 1),
                    )
                nc.vector.reduce_max(
                    out=neg_raw_top[:, j : j + 1], in_=raw_j[:], axis=FREE, negate=True
                )
                if j == 0 and b + 1 < blocks:
                    flip(b + 1, slabs)

            if first:
                neg_top = per_block.tile([P, banks], F32, name="neg_top")
                for lo, hi in ((0, 1), (1, banks - 1), (banks - 1, banks)):
                    nc.scalar.activation(
                        out=neg_top[:, lo:hi], in_=neg_raw_top[:, lo:hi], func=Act.Copy,
                        scale=inv_norm[b][:, 0:1],
                    )
                    if hi < banks:
                        exponentials(lo, neg_top[:, lo : lo + 1])
                for j in range(2, banks):
                    exponentials(j, neg_top[:, j : j + 1])
                neg_row_top = per_block.tile([P, 1], F32, name="neg_row_top")
                nc.vector.tensor_reduce(out=neg_row_top[:], in_=neg_top[:], axis=FREE, op=Alu.min)
                rescale = per_block.tile([P, banks], F32, name="rescale")
                nc.scalar.activation(
                    out=rescale[:], in_=neg_top[:], func=Act.Exp, bias=neg_row_top[:, 0:1], scale=-1.0
                )
                weighted = per_block.tile([P, banks], F32, name="weighted")
                total = per_block.tile([P, 1], F32, name="total")
                nc.vector.scalar_tensor_tensor(
                    out=weighted[:], in0=rescale[:], scalar=1.0, in1=bank_sum[:],
                    op0=Alu.mult, op1=Alu.mult, accum_out=total[:],
                )
                nc.vector.reciprocal(inv_total[:], total[:])

                factor = per_block.tile([P, banks], F32, name="factor")
                nc.scalar.activation(
                    out=factor[:], in_=rescale[:], func=Act.Copy, scale=inv_total[:, 0:1]
                )
                for j in range(banks):
                    if j < banks_a_piece:
                        nc.vector.tensor_scalar(
                            out=factor_spread_b[:, j * BANK : (j + 1) * BANK], in0=ones[:],
                            scalar1=rescale[:, j : j + 1], scalar2=inv_total[:, 0:1],
                            op0=Alu.mult, op1=Alu.mult,
                        )
                    else:
                        nc.scalar.activation(
                            out=factor_spread_b[:, j * BANK : (j + 1) * BANK], in_=ones[:],
                            func=Act.Copy, scale=factor[:, j : j + 1],
                        )
            else:
                neg_raw_row_top = per_block.tile([P, 1], F32, name="neg_raw_row_top")
                nc.vector.tensor_reduce(out=neg_raw_row_top[:], in_=neg_raw_top[:], axis=FREE, op=Alu.min)
                neg_row_top = per_block.tile([P, 1], F32, name="neg_row_top")
                nc.scalar.activation(
                    out=neg_row_top[:], in_=neg_raw_row_top[:], func=Act.Copy, scale=inv_norm[b][:, 0:1]
                )
                for j in range(banks):
                    exponentials(j, neg_row_top[:, 0:1])
                sum_copy = per_block.tile([P, banks], F32, name="sum_copy")
                total = per_block.tile([P, 1], F32, name="total")
                nc.scalar.activation(
                    out=sum_copy[:], in_=bank_sum[:], func=Act.Copy, accum_out=total[:]
                )
                log_total = per_block.tile([P, 1], F32, name="log_total")
                nc.scalar.activation(out=log_total[:], in_=total[:], func=Act.Ln)
                nc.scalar.activation(out=inv_total[:], in_=log_total[:], func=Act.Exp, scale=-1.0)
                for j in range(banks):
                    nc.scalar.activation(
                        out=factor_spread_b[:, j * BANK : (j + 1) * BANK], in_=ones[:],
                        func=Act.Copy, scale=inv_total[:, 0:1],
                    )
            expd.append(expd_b)
            factor_spread.append(factor_spread_b)

        for b in range(blocks):
            cuts = [0, FIRST_PIECE, n_cand] if b == 0 else [0, n_cand]
            for at, end in zip(cuts[:-1], cuts[1:]):
                nc.vector.tensor_tensor(
                    window[b][:].indirect(offsets[:, at // 16 : end // 16]),
                    expd[b][:, at:end],
                    factor_spread[b][:, at:end],
                    Alu.mult,
                )
            nc.sync.dma_start(out[b * P : (b + 1) * P, :], window[b][:])
